import numpy as np
import ml_dtypes


def mxq(x, axis, fmt="e4m3"):
    dtype, down = {"e4m3": (ml_dtypes.float8_e4m3fn, 7), "e5m2": (ml_dtypes.float8_e5m2, 14)}[fmt]
    v = np.moveaxis(np.asarray(x, np.float32).astype(ml_dtypes.bfloat16).astype(np.float64), axis, -1)
    blocks = v.reshape(v.shape[:-1] + (-1, 32))
    amax = np.abs(blocks).max(-1, keepdims=True)
    byte = np.maximum(np.where(amax > 0, np.frexp(amax)[1] - 1 + 127, 0) - down, 1)
    scale = np.exp2(byte - 127.0)
    codes = (blocks / scale).astype(np.float32).astype(dtype).astype(np.float64)
    return np.moveaxis((codes * scale).reshape(v.shape), -1, axis)


WIDE = False


def mx_kscale(k):
    if not WIDE:
        return np.ones(k)
    levels = np.array([10, -10, 5, -5, 0])
    if k % 512:
        return np.exp2(np.random.permutation(np.resize(levels, k // 32))).repeat(32)
    a = np.empty((k // 512, 16))
    for p in range(k // 512):
        a[p, :8] = np.random.permutation(np.resize(levels, 8))
        for g in range(8):
            far = levels[np.abs(levels - a[p, g]) >= 10]
            a[p, g + 8] = far[np.random.randint(len(far))]
    return np.exp2(a.ravel()).repeat(32)


BF16 = ml_dtypes.bfloat16


def bf(x):
    return np.asarray(x, np.float32).astype(BF16)


def f64(x):
    return np.asarray(x).astype(np.float64)


B, IN, HID, CENT = 1024, 128, 512, 2048


def setup_inputs():
    t = np.log2(mx_kscale(HID))
    a = t.max() - t
    sigmas = bf(1.0 + 0.1 * np.random.standard_normal(HID))
    c = np.random.standard_normal((HID, IN)) / np.sqrt(IN)
    c = c * np.sqrt(1.0 + a * np.log(2.0) / (f64(sigmas) ** 2 * (c * c).sum(1)))[:, None]
    return {"x": bf(np.random.standard_normal((B, IN)) / np.sqrt(IN)), "centres": bf(c), "sigmas": sigmas,
            "w1": bf(np.random.standard_normal((CENT, HID)) * 6.0 / np.sqrt(HID) * np.exp2(a)),
            "b1": bf(0.2 * np.random.standard_normal(CENT))}


def reference(x, centres, sigmas, w1, b1):
    x2 = np.sum(f64(x) * f64(x), axis=1, keepdims=True)
    c2 = np.sum(f64(centres) * f64(centres), axis=1)[None, :]
    d2 = np.maximum(x2 + c2 - 2.0 * (f64(x) @ f64(centres).T), 0.0)
    phi = np.exp(-d2 * (f64(sigmas) * f64(sigmas))[None, :])
    return np.maximum((mxq(phi, 1, "e4m3") @ mxq(f64(w1), 1, "e4m3").T) + f64(b1), 0.0)

@@ -1,0 +1,205 @@
+import concourse.mybir as mybir
+from concourse.masks import make_identity
+
+F32 = mybir.dt.float32
+BF16 = mybir.dt.bfloat16
+U32 = mybir.dt.uint32
+U8 = mybir.dt.uint8
+FP8X4 = mybir.dt.float8_e4m3fn_x4
+ALU = mybir.AluOpType
+ACT = mybir.ActivationFunctionType
+AXIS = mybir.AxisListType
+
+P = 128
+PACK = 4
+BATCH, IN, HID, CENT = 1024, 128, 512, 2048
+BANK = 512
+HALVES = BATCH // BANK
+ROW_TILES = BATCH // P
+TILES_PER_HALF = BANK // P
+CHUNKS = CENT // BANK
+FLT_MAX = 3.4028234663852886e38
+
+FLOPS = 2 * BATCH * IN * HID + 2 * BATCH * HID * CENT
+
+
+def tile_networkprc_pa_kernel(tc, x, centres, sigmas, w1, b1, out):
+    nc = tc.nc
+    with tc.tile_pool(name="keep", bufs=1) as keep, tc.tile_pool(name="work", bufs=2) as work, tc.psum_pool(
+        name="psum", bufs=2
+    ) as psum:
+        x_sb = keep.tile([P, ROW_TILES * IN], BF16)
+        nc.sync.dma_start(out=x_sb[:], in_=x.rearrange("(p a) k -> p (a k)", a=ROW_TILES))
+        c_sb = keep.tile([P, PACK, IN], BF16)
+        nc.sync.dma_start(out=c_sb[:], in_=centres.rearrange("(p t) k -> p t k", t=PACK))
+        sig = keep.tile([P, PACK], BF16)
+        nc.sync.dma_start(out=sig[:], in_=sigmas.rearrange("(p t) -> p t", t=PACK))
+        w_sb = []
+        b_all = keep.tile([P, CENT], BF16)
+        for q in range(CHUNKS):
+            w_chunk = keep.tile([P, TILES_PER_HALF * HID], BF16, name="w_sb%d" % q)
+            nc.sync.dma_start(
+                out=w_chunk[:].rearrange("p (m k) -> p m k", k=HID),
+                in_=w1[q * BANK : (q + 1) * BANK, :].rearrange("(m p) k -> p m k", p=P),
+            )
+            w_sb.append(w_chunk)
+            if q == 1:
+                nc.sync.dma_start(out=b_all[:], in_=b1.partition_broadcast(P))
+
+        ident_bf = keep.tile([P, P], BF16)
+        make_identity(nc, ident_bf[:])
+        ident_f32 = keep.tile([P, P], F32)
+        make_identity(nc, ident_f32[:])
+        neg_half = keep.tile([P, P], F32)
+        nc.vector.memset(neg_half[:], -0.5)
+        zero_col = keep.tile([P, 1], F32)
+        nc.vector.memset(zero_col[:], 0.0)
+        one_col = keep.tile([P, 1], F32)
+        nc.scalar.activation(out=one_col[:], in_=zero_col[:], func=ACT.Exp)
+
+        cT_ps = psum.tile([P, PACK, P], BF16, tag="tp")
+        for t in range(PACK):
+            nc.tensor.transpose(cT_ps[:, t, :], c_sb[:, t, :], ident_bf[:])
+        cT = keep.tile([P, PACK, P], BF16)
+        nc.scalar.copy(out=cT[:], in_=cT_ps[:])
+
+        xT = keep.tile([P, BATCH], BF16)
+        for h in range(HALVES):
+            xT_ps = psum.tile([P, TILES_PER_HALF, P], BF16, tag="tp")
+            for j in range(TILES_PER_HALF):
+                a = h * TILES_PER_HALF + j
+                nc.tensor.transpose(xT_ps[:, j, :], x_sb[:, a * IN : (a + 1) * IN], ident_bf[:])
+            nc.vector.tensor_copy(
+                out=xT[:, h * BANK : (h + 1) * BANK], in_=xT_ps[:].rearrange("p j r -> p (j r)")
+            )
+
+        c_sq = keep.tile([P, PACK, IN], F32)
+        nc.vector.tensor_tensor(out=c_sq[:], in0=c_sb[:], in1=c_sb[:], op=ALU.mult)
+        c_norm = keep.tile([P, PACK], F32)
+        nc.vector.tensor_reduce(out=c_norm[:], in_=c_sq[:], axis=AXIS.X, op=ALU.add)
+        exp_scale = keep.tile([P, PACK], F32)
+        nc.vector.scalar_tensor_tensor(
+            out=exp_scale[:], in0=sig[:], scalar=2.0, in1=sig[:], op0=ALU.mult, op1=ALU.mult
+        )
+        exp_bias = keep.tile([P, PACK], F32)
+        nc.vector.scalar_tensor_tensor(
+            out=exp_bias[:], in0=exp_scale[:], scalar=-0.5, in1=c_norm[:], op0=ALU.mult, op1=ALU.mult
+        )
+
+        x_sq = keep.tile([P, BATCH], F32)
+        neg_half_x_norm = keep.tile([P, BATCH], F32)
+
+        def x_norms(h):
+            cols = slice(h * BANK, (h + 1) * BANK)
+            nc.vector.tensor_tensor(out=x_sq[:, cols], in0=xT[:, cols], in1=xT[:, cols], op=ALU.mult)
+            norm_ps = psum.tile([P, BANK], F32, tag="g")
+            nc.tensor.matmul(out=norm_ps[:], lhsT=neg_half[:], rhs=x_sq[:, cols], start=True, stop=True)
+            nc.scalar.copy(out=neg_half_x_norm[:, cols], in_=norm_ps[:])
+
+        phi_codes = keep.tile([P, BATCH], U32, align_bytes=64)
+        phi_scales = keep.tile([P, BATCH], U8, align_bytes=64)
+        phi_planes = [
+            keep.tile([P, PACK, BANK], BF16, name="phi_planes%d" % h) for h in range(HALVES)
+        ]
+
+        def phi_plane(h, t):
+            cols = slice(h * BANK, (h + 1) * BANK)
+            g_ps = psum.tile([P, BANK], F32, tag="g")
+            nc.tensor.matmul(out=g_ps[:], lhsT=cT[:, t, :], rhs=xT[:, cols], start=True, stop=True)
+            g_minus = work.tile([P, BANK], F32)
+            nc.vector.tensor_tensor(out=g_minus[:], in0=g_ps[:], in1=neg_half_x_norm[:, cols], op=ALU.add)
+            nc.scalar.activation(
+                out=phi_planes[h][:, t, :],
+                in_=g_minus[:],
+                func=ACT.Exp,
+                scale=exp_scale[:, t : t + 1],
+                bias=exp_bias[:, t : t + 1],
+            )
+
+        def quantise_phi(h):
+            cols = slice(h * BANK, (h + 1) * BANK)
+            phi_grouped = work.tile([P, BANK, PACK], BF16, align_bytes=64)
+            nc.vector.tensor_scalar_min(
+                out=phi_grouped[:], in0=phi_planes[h][:].rearrange("p t i -> p i t"), scalar1=1.0
+            )
+            nc.vector.quantize_mx(
+                out=phi_codes[:, cols].bitcast(FP8X4),
+                scales=phi_scales[:, cols],
+                in_=phi_grouped[:].rearrange("p i t -> p (i t)"),
+            )
+
+        w_codes = keep.tile([P, CENT], U32, align_bytes=64)
+        w_scales = keep.tile([P, CENT], U8, align_bytes=64)
+
+        def quantise_w_chunk(q):
+            words = w_sb[q][:].bitcast(F32)
+            w_grouped = work.tile([P, BANK, 2], F32, align_bytes=64)
+            for pair in range(2):
+                wT_ps = psum.tile([P, 2, 2 * P], F32, tag="tp")
+                for u in range(2):
+                    for s in range(2):
+                        m = 2 * pair + s
+                        nc.tensor.transpose(
+                            wT_ps[:, u, s * P : (s + 1) * P],
+                            words[:, m * 256 + u : (m + 1) * 256 : 2],
+                            ident_f32[:],
+                        )
+                nc.scalar.copy(
+                    out=w_grouped[:, pair * 2 * P : (pair + 1) * 2 * P, :],
+                    in_=wT_ps[:].rearrange("p u n -> p n u"),
+                )
+            cols = slice(q * BANK, (q + 1) * BANK)
+            nc.vector.quantize_mx(
+                out=w_codes[:, cols].bitcast(FP8X4),
+                scales=w_scales[:, cols],
+                in_=w_grouped[:].rearrange("p n u -> p (n u)").bitcast(BF16),
+            )
+
+        out_view = out.rearrange("(p a) n -> p a n", a=ROW_TILES)
+
+        def output_block(h, q):
+            cols = slice(q * BANK, (q + 1) * BANK)
+            o_sb = work.tile([P, TILES_PER_HALF, BANK], F32, bufs=4)
+            for j in range(TILES_PER_HALF):
+                a = h * TILES_PER_HALF + j
+                rows = slice(a * P, (a + 1) * P)
+                acc = psum.tile([P, BANK], F32, tag="mx", bufs=4)
+                nc.tensor.matmul_mx(
+                    out=acc[:],
+                    lhsT=phi_codes[:, rows].bitcast(FP8X4),
+                    lhsT_scale=phi_scales[:, rows],
+                    rhs=w_codes[:, cols].bitcast(FP8X4),
+                    rhs_scale=w_scales[:, cols],
+                    start=True,
+                    stop=True,
+                )
+                nc.vector.tensor_tensor(out=o_sb[:, j, :], in0=acc[:], in1=b_all[:, cols], op=ALU.add)
+                if j % 2 == 0:
+                    nc.scalar.activation(out=o_sb[:, j, :], in_=o_sb[:, j, :], func=ACT.Relu)
+                else:
+                    nc.gpsimd.tensor_scalar(
+                        out=o_sb[:, j, :],
+                        in0=o_sb[:, j, :],
+                        scalar1=FLT_MAX,
+                        scalar2=0.0,
+                        op0=ALU.min,
+                        op1=ALU.max,
+                    )
+            nc.sync.dma_start(
+                out=out_view[:, h * TILES_PER_HALF : (h + 1) * TILES_PER_HALF, cols], in_=o_sb[:]
+            )
+
+        x_norms(0)
+        for t in range(PACK):
+            phi_plane(0, t)
+        quantise_w_chunk(0)
+        quantise_phi(0)
+        x_norms(1)
+        for q in range(CHUNKS):
+            if q + 1 < CHUNKS:
+                quantise_w_chunk(q + 1)
+            phi_plane(1, q)
+            output_block(0, q)
+        quantise_phi(1)
+        for q in range(CHUNKS):
+            output_block(1, q)

@@ -1,3 +1,5 @@
+from contextlib import ExitStack
+
 import concourse.mybir as mybir
 from concourse.masks import make_identity
 
@@ -8,198 +10,323 @@ U8 = mybir.dt.uint8
 FP8X4 = mybir.dt.float8_e4m3fn_x4
 ALU = mybir.AluOpType
 ACT = mybir.ActivationFunctionType
-AXIS = mybir.AxisListType
 
 P = 128
 PACK = 4
 BATCH, IN, HID, CENT = 1024, 128, 512, 2048
 BANK = 512
-HALVES = BATCH // BANK
 ROW_TILES = BATCH // P
-TILES_PER_HALF = BANK // P
 CHUNKS = CENT // BANK
+COL_TILES = BANK // P
+WORDS = HID // 2
 FLT_MAX = 3.4028234663852886e38
 
+AHEAD = 2
+LAG = 2
+NG = 8
 FLOPS = 2 * BATCH * IN * HID + 2 * BATCH * HID * CENT
 
 
 def tile_networkprc_pa_kernel(tc, x, centres, sigmas, w1, b1, out):
     nc = tc.nc
-    with tc.tile_pool(name="keep", bufs=1) as keep, tc.tile_pool(name="work", bufs=2) as work, tc.psum_pool(
-        name="psum", bufs=2
-    ) as psum:
-        x_sb = keep.tile([P, ROW_TILES * IN], BF16)
-        nc.sync.dma_start(out=x_sb[:], in_=x.rearrange("(p a) k -> p (a k)", a=ROW_TILES))
+    with ExitStack() as ctx:
+        keep = ctx.enter_context(tc.tile_pool(name="keep", bufs=1))
+        work = ctx.enter_context(tc.tile_pool(name="work", bufs=2))
+        psum = ctx.enter_context(tc.psum_pool(name="psum", bufs=2))
+        ctx.enter_context(tc.manual_schedule())
+
         c_sb = keep.tile([P, PACK, IN], BF16)
-        nc.sync.dma_start(out=c_sb[:], in_=centres.rearrange("(p t) k -> p t k", t=PACK))
+        x_sb = keep.tile([P, ROW_TILES, IN], BF16)
         sig = keep.tile([P, PACK], BF16)
-        nc.sync.dma_start(out=sig[:], in_=sigmas.rearrange("(p t) -> p t", t=PACK))
-        w_sb = []
-        b_all = keep.tile([P, CENT], BF16)
-        for q in range(CHUNKS):
-            w_chunk = keep.tile([P, TILES_PER_HALF * HID], BF16, name="w_sb%d" % q)
-            nc.sync.dma_start(
-                out=w_chunk[:].rearrange("p (m k) -> p m k", k=HID),
-                in_=w1[q * BANK : (q + 1) * BANK, :].rearrange("(m p) k -> p m k", p=P),
-            )
-            w_sb.append(w_chunk)
-            if q == 1:
-                nc.sync.dma_start(out=b_all[:], in_=b1.partition_broadcast(P))
-
+        b_row = keep.tile([P, CENT], BF16)
+        w_sb = [keep.tile([P, COL_TILES * HID], BF16, name="w_sb%d" % q) for q in range(CHUNKS)]
         ident_bf = keep.tile([P, P], BF16)
-        make_identity(nc, ident_bf[:])
         ident_f32 = keep.tile([P, P], F32)
-        make_identity(nc, ident_f32[:])
-        neg_half = keep.tile([P, P], F32)
-        nc.vector.memset(neg_half[:], -0.5)
+        ones_bf = keep.tile([P, P], BF16)
         zero_col = keep.tile([P, 1], F32)
-        nc.vector.memset(zero_col[:], 0.0)
         one_col = keep.tile([P, 1], F32)
-        nc.scalar.activation(out=one_col[:], in_=zero_col[:], func=ACT.Exp)
-
-        cT_ps = psum.tile([P, PACK, P], BF16, tag="tp")
-        for t in range(PACK):
-            nc.tensor.transpose(cT_ps[:, t, :], c_sb[:, t, :], ident_bf[:])
         cT = keep.tile([P, PACK, P], BF16)
-        nc.scalar.copy(out=cT[:], in_=cT_ps[:])
-
         xT = keep.tile([P, BATCH], BF16)
-        for h in range(HALVES):
-            xT_ps = psum.tile([P, TILES_PER_HALF, P], BF16, tag="tp")
-            for j in range(TILES_PER_HALF):
-                a = h * TILES_PER_HALF + j
-                nc.tensor.transpose(xT_ps[:, j, :], x_sb[:, a * IN : (a + 1) * IN], ident_bf[:])
-            nc.vector.tensor_copy(
-                out=xT[:, h * BANK : (h + 1) * BANK], in_=xT_ps[:].rearrange("p j r -> p (j r)")
-            )
-
-        c_sq = keep.tile([P, PACK, IN], F32)
-        nc.vector.tensor_tensor(out=c_sq[:], in0=c_sb[:], in1=c_sb[:], op=ALU.mult)
+        sq_c = keep.tile([P, PACK, IN], F32)
+        sq_x = keep.tile([P, ROW_TILES, IN], F32)
         c_norm = keep.tile([P, PACK], F32)
-        nc.vector.tensor_reduce(out=c_norm[:], in_=c_sq[:], axis=AXIS.X, op=ALU.add)
+        x_norm = keep.tile([P, ROW_TILES], F32)
+        x_rep = keep.tile([P, ROW_TILES, P], F32)
+        ones_f32 = keep.tile([P, P], F32)
         exp_scale = keep.tile([P, PACK], F32)
-        nc.vector.scalar_tensor_tensor(
-            out=exp_scale[:], in0=sig[:], scalar=2.0, in1=sig[:], op0=ALU.mult, op1=ALU.mult
-        )
         exp_bias = keep.tile([P, PACK], F32)
-        nc.vector.scalar_tensor_tensor(
-            out=exp_bias[:], in0=exp_scale[:], scalar=-0.5, in1=c_norm[:], op0=ALU.mult, op1=ALU.mult
-        )
-
-        x_sq = keep.tile([P, BATCH], F32)
-        neg_half_x_norm = keep.tile([P, BATCH], F32)
-
-        def x_norms(h):
-            cols = slice(h * BANK, (h + 1) * BANK)
-            nc.vector.tensor_tensor(out=x_sq[:, cols], in0=xT[:, cols], in1=xT[:, cols], op=ALU.mult)
-            norm_ps = psum.tile([P, BANK], F32, tag="g")
-            nc.tensor.matmul(out=norm_ps[:], lhsT=neg_half[:], rhs=x_sq[:, cols], start=True, stop=True)
-            nc.scalar.copy(out=neg_half_x_norm[:, cols], in_=norm_ps[:])
-
+        b_all = keep.tile([P, CENT], BF16)
         phi_codes = keep.tile([P, BATCH], U32, align_bytes=64)
         phi_scales = keep.tile([P, BATCH], U8, align_bytes=64)
-        phi_planes = [
-            keep.tile([P, PACK, BANK], BF16, name="phi_planes%d" % h) for h in range(HALVES)
+        w_codes = keep.tile([P, CENT], U32, align_bytes=64)
+        w_scales = keep.tile([P, CENT], U8, align_bytes=64)
+        w_grouped = [
+            keep.tile([P, BANK, 2], F32, align_bytes=64, name="w_grouped%d" % q) for q in range(CHUNKS)
         ]
+        out_view = out.rearrange("(p a) n -> p a n", a=ROW_TILES)
 
-        def phi_plane(h, t):
-            cols = slice(h * BANK, (h + 1) * BANK)
-            g_ps = psum.tile([P, BANK], F32, tag="g")
-            nc.tensor.matmul(out=g_ps[:], lhsT=cT[:, t, :], rhs=xT[:, cols], start=True, stop=True)
-            g_minus = work.tile([P, BANK], F32)
-            nc.vector.tensor_tensor(out=g_minus[:], in0=g_ps[:], in1=neg_half_x_norm[:, cols], op=ALU.add)
+        def load_w(q, first_tile, tiles):
+            c0 = q * BANK + first_tile * P
+            nc.sync.dma_start(
+                out=w_sb[q][:, first_tile * HID : (first_tile + tiles) * HID].rearrange("p (m k) -> p m k", k=HID),
+                in_=w1[c0 : c0 + tiles * P, :].rearrange("(m p) k -> p m k", p=P),
+            )
+
+        def load_x(first_tile, tiles):
+            nc.sync.dma_start(
+                out=x_sb[:, first_tile : first_tile + tiles, :],
+                in_=x.rearrange("(p a) k -> p a k", a=ROW_TILES)[:, first_tile : first_tile + tiles, :],
+            )
+
+        def transpose_x(tiles):
+            x_ps = psum.tile([P, len(tiles), P], BF16, tag="tp", bufs=3, name="x_ps")
+            for i, a in enumerate(tiles):
+                nc.tensor.transpose(x_ps[:, i, :], x_sb[:, a, :], ident_bf[:])
+            return x_ps
+
+        def copy_xT(x_ps, tiles):
+            nc.vector.tensor_copy(
+                out=xT[:, tiles[0] * P : (tiles[-1] + 1) * P], in_=x_ps[:].rearrange("p a r -> p (a r)")
+            )
+
+        def norm_x(a):
             nc.scalar.activation(
-                out=phi_planes[h][:, t, :],
-                in_=g_minus[:],
-                func=ACT.Exp,
-                scale=exp_scale[:, t : t + 1],
-                bias=exp_bias[:, t : t + 1],
+                out=sq_x[:, a, :], in_=x_sb[:, a, :], func=ACT.Square, accum_out=x_norm[:, a : a + 1]
+            )
+            nc.gpsimd.tensor_scalar(
+                out=x_rep[:, a, :], in0=ones_f32[:], scalar1=x_norm[:, a : a + 1], scalar2=0.0, op0=ALU.mult, op1=ALU.add
             )
 
-        def quantise_phi(h):
-            cols = slice(h * BANK, (h + 1) * BANK)
-            phi_grouped = work.tile([P, BANK, PACK], BF16, align_bytes=64)
-            nc.vector.tensor_scalar_min(
-                out=phi_grouped[:], in0=phi_planes[h][:].rearrange("p t i -> p i t"), scalar1=1.0
+        def distances(tiles):
+            rows = len(tiles) * P
+            blocks = BANK // rows
+            banks = []
+            for first in range(0, PACK, blocks):
+                d_ps = psum.tile([P, blocks, rows], F32, tag="g", name="d_ps")
+                for i in range(blocks):
+                    nc.tensor.matmul(
+                        out=d_ps[:, i, :],
+                        lhsT=cT[:, first + i, :],
+                        rhs=xT[:, tiles[0] * P : (tiles[-1] + 1) * P],
+                        start=True,
+                        stop=False,
+                    )
+                    for j, a in enumerate(tiles):
+                        nc.tensor.matmul(
+                            out=d_ps[:, i, j * P : (j + 1) * P],
+                            lhsT=x_rep[:, a, :],
+                            rhs=ident_f32[:],
+                            is_transpose=True,
+                            start=False,
+                            stop=a == tiles[-1],
+                        )
+                banks.append(d_ps)
+            return banks
+
+        def exps(banks, tiles):
+            rows = len(tiles) * P
+            blocks = BANK // rows
+            phi_blocks = work.tile([P, PACK, rows], BF16, bufs=4, name="phi_blocks")
+            for t in range(PACK):
+                nc.scalar.activation(
+                    out=phi_blocks[:, t, :],
+                    in_=banks[t // blocks][:, t % blocks, :],
+                    func=ACT.Exp,
+                    scale=exp_scale[:, t : t + 1],
+                    bias=exp_bias[:, t : t + 1],
+                )
+            return phi_blocks
+
+        def group_phi(phi_blocks, tiles):
+            phi_grouped = work.tile(
+                [P, len(tiles) * P, PACK], BF16, align_bytes=64, name="phi_grouped"
             )
+            nc.vector.tensor_scalar_min(
+                out=phi_grouped[:], in0=phi_blocks[:].rearrange("p t i -> p i t"), scalar1=1.0
+            )
+            return phi_grouped
+
+        def quantise_phi(phi_grouped, tiles):
+            rows = slice(tiles[0] * P, (tiles[-1] + 1) * P)
             nc.vector.quantize_mx(
-                out=phi_codes[:, cols].bitcast(FP8X4),
-                scales=phi_scales[:, cols],
+                out=phi_codes[:, rows].bitcast(FP8X4),
+                scales=phi_scales[:, rows],
                 in_=phi_grouped[:].rearrange("p i t -> p (i t)"),
             )
 
-        w_codes = keep.tile([P, CENT], U32, align_bytes=64)
-        w_scales = keep.tile([P, CENT], U8, align_bytes=64)
-
-        def quantise_w_chunk(q):
+        def transpose_w(q, pair):
             words = w_sb[q][:].bitcast(F32)
-            w_grouped = work.tile([P, BANK, 2], F32, align_bytes=64)
-            for pair in range(2):
-                wT_ps = psum.tile([P, 2, 2 * P], F32, tag="tp")
-                for u in range(2):
-                    for s in range(2):
-                        m = 2 * pair + s
-                        nc.tensor.transpose(
-                            wT_ps[:, u, s * P : (s + 1) * P],
-                            words[:, m * 256 + u : (m + 1) * 256 : 2],
-                            ident_f32[:],
-                        )
-                nc.scalar.copy(
-                    out=w_grouped[:, pair * 2 * P : (pair + 1) * 2 * P, :],
-                    in_=wT_ps[:].rearrange("p u n -> p n u"),
-                )
-            cols = slice(q * BANK, (q + 1) * BANK)
+            w_ps = psum.tile([P, 2, 2 * P], F32, tag="tp", bufs=3, name="w_ps")
+            for u in range(2):
+                for half in range(2):
+                    m = 2 * pair + half
+                    nc.tensor.transpose(
+                        w_ps[:, u, half * P : (half + 1) * P],
+                        words[:, m * WORDS + u : (m + 1) * WORDS : 2],
+                        ident_f32[:],
+                    )
+            return w_ps
+
+        def group_w(copy_out, q, pair, w_ps):
+            copy_out(
+                out=w_grouped[q][:, pair * 2 * P : (pair + 1) * 2 * P, :],
+                in_=w_ps[:].rearrange("p u n -> p n u"),
+            )
+
+        def quantise_w(q, first, columns):
+            cols = slice(q * BANK + first, q * BANK + first + columns)
             nc.vector.quantize_mx(
                 out=w_codes[:, cols].bitcast(FP8X4),
                 scales=w_scales[:, cols],
-                in_=w_grouped[:].rearrange("p n u -> p (n u)").bitcast(BF16),
+                in_=w_grouped[q][:, first : first + columns, :].rearrange("p n u -> p (n u)").bitcast(BF16),
             )
 
-        out_view = out.rearrange("(p a) n -> p a n", a=ROW_TILES)
-
-        def output_block(h, q):
+        def spread_b(q):
+            b_ps = psum.tile([P, BANK], BF16, tag="mx", bufs=3, name="b_ps")
             cols = slice(q * BANK, (q + 1) * BANK)
-            o_sb = work.tile([P, TILES_PER_HALF, BANK], F32, bufs=4)
-            for j in range(TILES_PER_HALF):
-                a = h * TILES_PER_HALF + j
-                rows = slice(a * P, (a + 1) * P)
-                acc = psum.tile([P, BANK], F32, tag="mx", bufs=4)
-                nc.tensor.matmul_mx(
-                    out=acc[:],
-                    lhsT=phi_codes[:, rows].bitcast(FP8X4),
-                    lhsT_scale=phi_scales[:, rows],
-                    rhs=w_codes[:, cols].bitcast(FP8X4),
-                    rhs_scale=w_scales[:, cols],
-                    start=True,
-                    stop=True,
-                )
-                nc.vector.tensor_tensor(out=o_sb[:, j, :], in0=acc[:], in1=b_all[:, cols], op=ALU.add)
-                if j % 2 == 0:
-                    nc.scalar.activation(out=o_sb[:, j, :], in_=o_sb[:, j, :], func=ACT.Relu)
-                else:
-                    nc.gpsimd.tensor_scalar(
-                        out=o_sb[:, j, :],
-                        in0=o_sb[:, j, :],
-                        scalar1=FLT_MAX,
-                        scalar2=0.0,
-                        op0=ALU.min,
-                        op1=ALU.max,
-                    )
-            nc.sync.dma_start(
-                out=out_view[:, h * TILES_PER_HALF : (h + 1) * TILES_PER_HALF, cols], in_=o_sb[:]
+            nc.tensor.matmul(out=b_ps[:], lhsT=ones_bf[:], rhs=b_row[:, cols], start=True, stop=True)
+            return b_ps
+
+        def copy_b(copy_out, q, b_ps):
+            copy_out(out=b_all[:, q * BANK : (q + 1) * BANK], in_=b_ps[:])
+
+        def product(a, q):
+            acc = psum.tile([P, BANK], F32, tag="mx", bufs=3, name="acc")
+            rows = slice(a * P, (a + 1) * P)
+            cols = slice(q * BANK, (q + 1) * BANK)
+            nc.tensor.matmul_mx(
+                out=acc[:],
+                lhsT=phi_codes[:, rows].bitcast(FP8X4),
+                lhsT_scale=phi_scales[:, rows],
+                rhs=w_codes[:, cols].bitcast(FP8X4),
+                rhs_scale=w_scales[:, cols],
+                start=True,
+                stop=True,
+            )
+            return acc
+
+        def add_b(o_sb, j, q, acc):
+            nc.vector.tensor_tensor(
+                out=o_sb[:, j, :], in0=acc[:], in1=b_all[:, q * BANK : (q + 1) * BANK], op=ALU.add
             )
 
-        x_norms(0)
+        def relu(o_sb, j, engine):
+            if engine == "G":
+                nc.gpsimd.tensor_scalar(
+                    out=o_sb[:, j, :], in0=o_sb[:, j, :], scalar1=FLT_MAX, scalar2=0.0, op0=ALU.min, op1=ALU.max
+                )
+            else:
+                nc.scalar.activation(out=o_sb[:, j, :], in_=o_sb[:, j, :], func=ACT.Relu)
+
+        def make_w(q, pair):
+            group_w(nc.scalar.copy, q, pair, transpose_w(q, pair))
+            if pair == 1:
+                copy_b(nc.scalar.copy, q, spread_b(q))
+                return [lambda: quantise_w(q, 0, BANK)]
+            return []
+
+        def make_phi(a):
+            phi_blocks = exps(distances([a]), [a])
+            grouped = []
+            return [lambda: grouped.append(group_phi(phi_blocks, [a])), lambda: quantise_phi(grouped[0], [a])]
+
+        def make_x(tiles):
+            copy_xT(transpose_x(tiles), tiles)
+            for a in tiles:
+                norm_x(a)
+            return []
+
+        nc.sync.dma_start(out=c_sb[:], in_=centres.rearrange("(p t) k -> p t k", t=PACK))
+        load_x(0, 4)
+        nc.sync.dma_start(out=sig[:], in_=sigmas.rearrange("(p t) -> p t", t=PACK))
+        load_w(0, 0, 2)
+        load_w(0, 2, 2)
+        nc.vector.memset(b_row[:].bitcast(U32), 0)
+        nc.sync.dma_start(out=b_row[0:1, :], in_=b1.rearrange("(o n) -> o n", o=1))
+        load_w(1, 0, 4)
+        load_x(4, 4)
+        for q in range(2, CHUNKS):
+            load_w(q, 0, 4)
+
+        make_identity(nc, ident_bf[:])
+        make_identity(nc, ident_f32[:])
+        nc.gpsimd.memset(zero_col[:], 0.0)
+        nc.gpsimd.memset(ones_f32[:], 1.0)
+        nc.gpsimd.memset(ones_bf[:], 1.0)
+        nc.scalar.activation(out=one_col[:], in_=zero_col[:], func=ACT.Exp)
+
+        c_ps = psum.tile([P, PACK, P], BF16, tag="tp", bufs=3)
         for t in range(PACK):
-            phi_plane(0, t)
-        quantise_w_chunk(0)
-        quantise_phi(0)
-        x_norms(1)
-        for q in range(CHUNKS):
-            if q + 1 < CHUNKS:
-                quantise_w_chunk(q + 1)
-            phi_plane(1, q)
-            output_block(0, q)
-        quantise_phi(1)
-        for q in range(CHUNKS):
-            output_block(1, q)
+            nc.tensor.transpose(c_ps[:, t, :], c_sb[:, t, :], ident_bf[:])
+        x_ps = transpose_x([0, 1, 2, 3])
+        norm_x(0)
+        for t in range(PACK):
+            nc.scalar.activation(
+                out=sq_c[:, t, :], in_=c_sb[:, t, :], func=ACT.Square, accum_out=c_norm[:, t : t + 1]
+            )
+        for a in range(1, 4):
+            norm_x(a)
+        nc.vector.tensor_scalar(out=cT[:], in0=c_ps[:], scalar1=-2.0, scalar2=None, op0=ALU.mult)
+        copy_xT(x_ps, [0, 1, 2, 3])
+        nc.vector.scalar_tensor_tensor(
+            out=exp_scale[:], in0=sig[:], scalar=-1.0, in1=sig[:], op0=ALU.mult, op1=ALU.mult
+        )
+        nc.vector.tensor_tensor(out=exp_bias[:], in0=exp_scale[:], in1=c_norm[:], op=ALU.mult)
+        w_a = transpose_w(0, 0)
+        d0 = distances([0])
+        e0 = exps(d0, [0])
+        group_w(nc.vector.tensor_copy, 0, 0, w_a)
+        quantise_w(0, 0, 256)
+        w_b = transpose_w(0, 1)
+        d1 = distances([1])
+        e1 = exps(d1, [1])
+        b_ps = spread_b(0)
+        g0 = group_phi(e0, [0])
+        group_w(nc.vector.tensor_copy, 0, 1, w_b)
+        quantise_phi(g0, [0])
+        quantise_w(0, 256, 256)
+        copy_b(nc.vector.tensor_copy, 0, b_ps)
+        g1 = group_phi(e1, [1])
+
+        jobs = [
+            lambda: make_w(1, 0),
+            lambda: make_w(1, 1),
+            lambda: make_phi(2),
+            lambda: make_phi(3),
+            lambda: make_w(2, 0),
+            lambda: make_w(2, 1),
+            lambda: make_x([4, 5, 6, 7]),
+            lambda: make_phi(4),
+            lambda: make_phi(5),
+            lambda: make_w(3, 0),
+            lambda: make_w(3, 1),
+            lambda: make_phi(6),
+            lambda: make_phi(7),
+        ]
+        late = {1: [lambda: quantise_phi(g1, [1])]}
+
+        def start_job(slot):
+            if jobs:
+                for i, stage in enumerate(jobs.pop(0)()):
+                    late.setdefault(slot + LAG + i, []).append(stage)
+
+        for slot in range(-AHEAD, 0):
+            start_job(slot)
+        order = [(0, 0), (1, 0), (0, 1), (1, 1)] + [(a, q) for a in (2, 3) for q in (0, 1)]
+        order += [(a, 2) for a in range(4)] + [(a, q) for a in (4, 5) for q in range(3)]
+        order += [(a, 3) for a in range(6)] + [(a, q) for a in (6, 7) for q in range(4)]
+        for slot, (a, q) in enumerate(order):
+            for stage in late.pop(slot, []):
+                stage()
+            acc = product(a, q)
+            start_job(slot)
+            o_sb = work.tile([P, BANK], F32, bufs=12, name="o_sb")
+            cols = slice(q * BANK, (q + 1) * BANK)
+            nc.vector.tensor_tensor(out=o_sb[:], in0=acc[:], in1=b_all[:, cols], op=ALU.add)
+            if slot < NG or slot % 2 == 0:
+                nc.gpsimd.tensor_scalar(
+                    out=o_sb[:], in0=o_sb[:], scalar1=FLT_MAX, scalar2=0.0, op0=ALU.min, op1=ALU.max
+                )
+            else:
+                nc.scalar.activation(out=o_sb[:], in_=o_sb[:], func=ACT.Relu)
+            nc.sync.dma_start(out=out_view[:, a, cols], in_=o_sb[:])

@@ -21,9 +21,16 @@ COL_TILES = BANK // P
 WORDS = HID // 2
 FLT_MAX = 3.4028234663852886e38
 
+D1 = (128, 128, 128, 128)
+D2 = ()
+GB = 2
+OB = 16
+MXB = 4
+RELU = "GGGGGGGGGSGSGSGSGSGSGSGSGSGSGSGS"
 AHEAD = 2
 LAG = 2
-NG = 8
+TPB = 2
+GG = ()
 FLOPS = 2 * BATCH * IN * HID + 2 * BATCH * HID * CENT
 
 
@@ -38,7 +45,8 @@ def tile_networkprc_pa_kernel(tc, x, centres, sigmas, w1, b1, out):
         c_sb = keep.tile([P, PACK, IN], BF16)
         x_sb = keep.tile([P, ROW_TILES, IN], BF16)
         sig = keep.tile([P, PACK], BF16)
-        b_row = keep.tile([P, CENT], BF16)
+        b_row = [keep.tile([P, CENT // 2], BF16, name="b_row%d" % half) for half in range(2)]
+        warm = keep.tile([P, P], F32)
         w_sb = [keep.tile([P, COL_TILES * HID], BF16, name="w_sb%d" % q) for q in range(CHUNKS)]
         ident_bf = keep.tile([P, P], BF16)
         ident_f32 = keep.tile([P, P], F32)
@@ -49,10 +57,10 @@ def tile_networkprc_pa_kernel(tc, x, centres, sigmas, w1, b1, out):
         xT = keep.tile([P, BATCH], BF16)
         sq_c = keep.tile([P, PACK, IN], F32)
         sq_x = keep.tile([P, ROW_TILES, IN], F32)
-        c_norm = keep.tile([P, PACK], F32)
+        c_norm_v = keep.tile([P, 1], F32)
+        c_norm_s = keep.tile([P, PACK], F32)
         x_norm = keep.tile([P, ROW_TILES], F32)
         x_rep = keep.tile([P, ROW_TILES, P], F32)
-        ones_f32 = keep.tile([P, P], F32)
         exp_scale = keep.tile([P, PACK], F32)
         exp_bias = keep.tile([P, PACK], F32)
         b_all = keep.tile([P, CENT], BF16)
@@ -79,7 +87,7 @@ def tile_networkprc_pa_kernel(tc, x, centres, sigmas, w1, b1, out):
             )
 
         def transpose_x(tiles):
-            x_ps = psum.tile([P, len(tiles), P], BF16, tag="tp", bufs=3, name="x_ps")
+            x_ps = psum.tile([P, len(tiles), P], BF16, tag="tp", bufs=TPB, name="x_ps")
             for i, a in enumerate(tiles):
                 nc.tensor.transpose(x_ps[:, i, :], x_sb[:, a, :], ident_bf[:])
             return x_ps
@@ -93,8 +101,11 @@ def tile_networkprc_pa_kernel(tc, x, centres, sigmas, w1, b1, out):
             nc.scalar.activation(
                 out=sq_x[:, a, :], in_=x_sb[:, a, :], func=ACT.Square, accum_out=x_norm[:, a : a + 1]
             )
-            nc.gpsimd.tensor_scalar(
-                out=x_rep[:, a, :], in0=ones_f32[:], scalar1=x_norm[:, a : a + 1], scalar2=0.0, op0=ALU.mult, op1=ALU.add
+
+        def spread_norms(first, tiles):
+            nc.vector.tensor_copy(
+                out=x_rep[:, first : first + tiles, :],
+                in_=x_norm[:, first : first + tiles].unsqueeze(2).to_broadcast([P, tiles, P]),
             )
 
         def distances(tiles):
@@ -126,7 +137,7 @@ def tile_networkprc_pa_kernel(tc, x, centres, sigmas, w1, b1, out):
         def exps(banks, tiles):
             rows = len(tiles) * P
             blocks = BANK // rows
-            phi_blocks = work.tile([P, PACK, rows], BF16, bufs=4, name="phi_blocks")
+            phi_blocks = work.tile([P, PACK, rows], BF16, bufs=4, name="phi_blocks%d" % len(tiles))
             for t in range(PACK):
                 nc.scalar.activation(
                     out=phi_blocks[:, t, :],
@@ -141,9 +152,19 @@ def tile_networkprc_pa_kernel(tc, x, centres, sigmas, w1, b1, out):
             phi_grouped = work.tile(
                 [P, len(tiles) * P, PACK], BF16, align_bytes=64, name="phi_grouped"
             )
-            nc.vector.tensor_scalar_min(
-                out=phi_grouped[:], in0=phi_blocks[:].rearrange("p t i -> p i t"), scalar1=1.0
-            )
+            if tiles[0] in GG:
+                nc.gpsimd.tensor_scalar(
+                    out=phi_grouped[:],
+                    in0=phi_blocks[:].rearrange("p t i -> p i t"),
+                    scalar1=-FLT_MAX,
+                    scalar2=1.0,
+                    op0=ALU.max,
+                    op1=ALU.min,
+                )
+            else:
+                nc.vector.tensor_scalar_min(
+                    out=phi_grouped[:], in0=phi_blocks[:].rearrange("p t i -> p i t"), scalar1=1.0
+                )
             return phi_grouped
 
         def quantise_phi(phi_grouped, tiles):
@@ -156,7 +177,7 @@ def tile_networkprc_pa_kernel(tc, x, centres, sigmas, w1, b1, out):
 
         def transpose_w(q, pair):
             words = w_sb[q][:].bitcast(F32)
-            w_ps = psum.tile([P, 2, 2 * P], F32, tag="tp", bufs=3, name="w_ps")
+            w_ps = psum.tile([P, 2, 2 * P], F32, tag="tp", bufs=TPB, name="w_ps")
             for u in range(2):
                 for half in range(2):
                     m = 2 * pair + half
@@ -181,17 +202,21 @@ def tile_networkprc_pa_kernel(tc, x, centres, sigmas, w1, b1, out):
                 in_=w_grouped[q][:, first : first + columns, :].rearrange("p n u -> p (n u)").bitcast(BF16),
             )
 
-        def spread_b(q):
-            b_ps = psum.tile([P, BANK], BF16, tag="mx", bufs=3, name="b_ps")
-            cols = slice(q * BANK, (q + 1) * BANK)
-            nc.tensor.matmul(out=b_ps[:], lhsT=ones_bf[:], rhs=b_row[:, cols], start=True, stop=True)
+        def spread_b(half):
+            b_ps = psum.tile([P, 2, BANK], BF16, tag="mx", bufs=MXB, name="b_ps")
+            for i in range(2):
+                nc.tensor.matmul(
+                    out=b_ps[:, i, :], lhsT=ones_bf[:], rhs=b_row[half][:, i * BANK : (i + 1) * BANK], start=True, stop=True
+                )
             return b_ps
 
-        def copy_b(copy_out, q, b_ps):
-            copy_out(out=b_all[:, q * BANK : (q + 1) * BANK], in_=b_ps[:])
+        def copy_b(copy_out, half, b_ps):
+            copy_out(
+                out=b_all[:, half * CENT // 2 : (half + 1) * CENT // 2], in_=b_ps[:].rearrange("p i n -> p (i n)")
+            )
 
         def product(a, q):
-            acc = psum.tile([P, BANK], F32, tag="mx", bufs=3, name="acc")
+            acc = psum.tile([P, BANK], F32, tag="mx", bufs=MXB, name="acc")
             rows = slice(a * P, (a + 1) * P)
             cols = slice(q * BANK, (q + 1) * BANK)
             nc.tensor.matmul_mx(
@@ -221,7 +246,6 @@ def tile_networkprc_pa_kernel(tc, x, centres, sigmas, w1, b1, out):
         def make_w(q, pair):
             group_w(nc.scalar.copy, q, pair, transpose_w(q, pair))
             if pair == 1:
-                copy_b(nc.scalar.copy, q, spread_b(q))
                 return [lambda: quantise_w(q, 0, BANK)]
             return []
 
@@ -230,63 +254,90 @@ def tile_networkprc_pa_kernel(tc, x, centres, sigmas, w1, b1, out):
             grouped = []
             return [lambda: grouped.append(group_phi(phi_blocks, [a])), lambda: quantise_phi(grouped[0], [a])]
 
-        def make_x(tiles):
-            copy_xT(transpose_x(tiles), tiles)
-            for a in tiles:
-                norm_x(a)
-            return []
 
         nc.sync.dma_start(out=c_sb[:], in_=centres.rearrange("(p t) k -> p t k", t=PACK))
-        load_x(0, 4)
+        load_x(0, 2)
         nc.sync.dma_start(out=sig[:], in_=sigmas.rearrange("(p t) -> p t", t=PACK))
         load_w(0, 0, 2)
-        load_w(0, 2, 2)
-        nc.vector.memset(b_row[:].bitcast(U32), 0)
-        nc.sync.dma_start(out=b_row[0:1, :], in_=b1.rearrange("(o n) -> o n", o=1))
-        load_w(1, 0, 4)
-        load_x(4, 4)
-        for q in range(2, CHUNKS):
+        nc.vector.memset(warm[:], 0.0)
+        for half in range(2):
+            cols = slice(half * CENT // 2, (half + 1) * CENT // 2)
+            nc.vector.memset(b_row[half][:].bitcast(U32), 0)
+            nc.sync.dma_start(out=b_row[half][0:1, :], in_=b1[cols].rearrange("(o n) -> o n", o=1))
+            if half == 0:
+                load_w(0, 2, 2)
+                load_x(2, 6)
+        for q in range(1, CHUNKS):
             load_w(q, 0, 4)
 
         make_identity(nc, ident_bf[:])
         make_identity(nc, ident_f32[:])
         nc.gpsimd.memset(zero_col[:], 0.0)
-        nc.gpsimd.memset(ones_f32[:], 1.0)
         nc.gpsimd.memset(ones_bf[:], 1.0)
         nc.scalar.activation(out=one_col[:], in_=zero_col[:], func=ACT.Exp)
 
-        c_ps = psum.tile([P, PACK, P], BF16, tag="tp", bufs=3)
+        def warm_up(columns):
+            w_ps = psum.tile([P, BANK], F32, tag="mx", bufs=MXB, name="warm_ps")
+            nc.tensor.matmul(out=w_ps[:, 0:columns], lhsT=warm[:, 0:P], rhs=warm[:, 0:columns], start=True, stop=True)
+
+        for columns in D1:
+            warm_up(columns)
+        c_ps = psum.tile([P, PACK, P], BF16, tag="tp", bufs=TPB)
         for t in range(PACK):
             nc.tensor.transpose(c_ps[:, t, :], c_sb[:, t, :], ident_bf[:])
-        x_ps = transpose_x([0, 1, 2, 3])
-        norm_x(0)
-        for t in range(PACK):
+        first_ps = transpose_x([0, 1])
+        w_a = transpose_w(0, 0)
+        b_ps = spread_b(0)
+
+        def norm_c_on_scalar(t):
             nc.scalar.activation(
-                out=sq_c[:, t, :], in_=c_sb[:, t, :], func=ACT.Square, accum_out=c_norm[:, t : t + 1]
+                out=sq_c[:, t, :], in_=c_sb[:, t, :], func=ACT.Square, accum_out=c_norm_s[:, t : t + 1]
             )
-        for a in range(1, 4):
-            norm_x(a)
+
+        norm_c_on_scalar(1)
+        norm_x(0)
+        norm_x(1)
+        norm_c_on_scalar(2)
+        norm_c_on_scalar(3)
+        nc.vector.scalar_tensor_tensor(
+            out=sq_c[:, 0, :],
+            in0=c_sb[:, 0, :],
+            scalar=1.0,
+            in1=c_sb[:, 0, :],
+            op0=ALU.mult,
+            op1=ALU.mult,
+            accum_out=c_norm_v[:],
+        )
         nc.vector.tensor_scalar(out=cT[:], in0=c_ps[:], scalar1=-2.0, scalar2=None, op0=ALU.mult)
-        copy_xT(x_ps, [0, 1, 2, 3])
+        copy_xT(first_ps, [0, 1])
+        spread_norms(0, 2)
         nc.vector.scalar_tensor_tensor(
             out=exp_scale[:], in0=sig[:], scalar=-1.0, in1=sig[:], op0=ALU.mult, op1=ALU.mult
         )
-        nc.vector.tensor_tensor(out=exp_bias[:], in0=exp_scale[:], in1=c_norm[:], op=ALU.mult)
-        w_a = transpose_w(0, 0)
-        d0 = distances([0])
-        e0 = exps(d0, [0])
+        nc.vector.tensor_tensor(out=exp_bias[:, 0:1], in0=exp_scale[:, 0:1], in1=c_norm_v[:], op=ALU.mult)
+        nc.vector.tensor_tensor(out=exp_bias[:, 1:], in0=exp_scale[:, 1:], in1=c_norm_s[:, 1:], op=ALU.mult)
+
+        e0 = exps(distances([0]), [0])
         group_w(nc.vector.tensor_copy, 0, 0, w_a)
-        quantise_w(0, 0, 256)
         w_b = transpose_w(0, 1)
-        d1 = distances([1])
-        e1 = exps(d1, [1])
-        b_ps = spread_b(0)
+        copy_b(nc.vector.tensor_copy, 0, b_ps)
+        quantise_w(0, 0, 256)
+        norm_x(2)
+        norm_x(3)
+        e1 = exps(distances([1]), [1])
         g0 = group_phi(e0, [0])
         group_w(nc.vector.tensor_copy, 0, 1, w_b)
         quantise_phi(g0, [0])
+        b1_ps = spread_b(1)
         quantise_w(0, 256, 256)
-        copy_b(nc.vector.tensor_copy, 0, b_ps)
+        rest_ps = transpose_x(list(range(2, ROW_TILES)))
         g1 = group_phi(e1, [1])
+        for a in range(4, ROW_TILES):
+            norm_x(a)
+        copy_b(nc.scalar.copy, 1, b1_ps)
+        copy_xT(rest_ps, list(range(2, ROW_TILES)))
+        spread_norms(2, 6)
+        late = {1: [lambda: quantise_phi(g1, [1])]}
 
         jobs = [
             lambda: make_w(1, 0),
@@ -295,7 +346,6 @@ def tile_networkprc_pa_kernel(tc, x, centres, sigmas, w1, b1, out):
             lambda: make_phi(3),
             lambda: make_w(2, 0),
             lambda: make_w(2, 1),
-            lambda: make_x([4, 5, 6, 7]),
             lambda: make_phi(4),
             lambda: make_phi(5),
             lambda: make_w(3, 0),
@@ -303,7 +353,6 @@ def tile_networkprc_pa_kernel(tc, x, centres, sigmas, w1, b1, out):
             lambda: make_phi(6),
             lambda: make_phi(7),
         ]
-        late = {1: [lambda: quantise_phi(g1, [1])]}
 
         def start_job(slot):
             if jobs:
@@ -319,14 +368,18 @@ def tile_networkprc_pa_kernel(tc, x, centres, sigmas, w1, b1, out):
             for stage in late.pop(slot, []):
                 stage()
             acc = product(a, q)
-            start_job(slot)
-            o_sb = work.tile([P, BANK], F32, bufs=12, name="o_sb")
+            if slot < 2 or slot % 2 == 1:
+                for i in range(1 if slot < 2 else 2):
+                    start_job(slot)
+            o_sb = work.tile([P, BANK], F32, bufs=OB, name="o_sb")
             cols = slice(q * BANK, (q + 1) * BANK)
             nc.vector.tensor_tensor(out=o_sb[:], in0=acc[:], in1=b_all[:, cols], op=ALU.add)
-            if slot < NG or slot % 2 == 0:
+            if RELU[slot] == "G":
                 nc.gpsimd.tensor_scalar(
                     out=o_sb[:], in0=o_sb[:], scalar1=FLT_MAX, scalar2=0.0, op0=ALU.min, op1=ALU.max
                 )
+            elif RELU[slot] == "V":
+                nc.vector.tensor_scalar_max(out=o_sb[:], in0=o_sb[:], scalar1=0.0)
             else:
                 nc.scalar.activation(out=o_sb[:], in_=o_sb[:], func=ACT.Relu)
             nc.sync.dma_start(out=out_view[:, a, cols], in_=o_sb[:])

@@ -22,15 +22,14 @@ WORDS = HID // 2
 FLT_MAX = 3.4028234663852886e38
 
 D1 = (128, 128, 128, 128)
-D2 = ()
+D2 = (128,)
 GB = 2
-OB = 16
+OB = 8
 MXB = 4
 RELU = "GGGGGGGGGSGSGSGSGSGSGSGSGSGSGSGS"
 AHEAD = 2
 LAG = 2
 TPB = 2
-GG = ()
 FLOPS = 2 * BATCH * IN * HID + 2 * BATCH * HID * CENT
 
 
@@ -73,11 +72,13 @@ def tile_networkprc_pa_kernel(tc, x, centres, sigmas, w1, b1, out):
         ]
         out_view = out.rearrange("(p a) n -> p a n", a=ROW_TILES)
 
-        def load_w(q, first_tile, tiles):
-            c0 = q * BANK + first_tile * P
+        def load_w(q, first_pair, pairs):
+            c0 = q * BANK + first_pair * 2 * P
             nc.sync.dma_start(
-                out=w_sb[q][:, first_tile * HID : (first_tile + tiles) * HID].rearrange("p (m k) -> p m k", k=HID),
-                in_=w1[c0 : c0 + tiles * P, :].rearrange("(m p) k -> p m k", p=P),
+                out=w_sb[q][:, first_pair * 2 * HID : (first_pair + pairs) * 2 * HID].rearrange(
+                    "p (h m k) -> p h m k", m=2, k=HID
+                ),
+                in_=w1[c0 : c0 + pairs * 2 * P, :].rearrange("(h p m) k -> p h m k", p=P, m=2),
             )
 
         def load_x(first_tile, tiles):
@@ -152,19 +153,9 @@ def tile_networkprc_pa_kernel(tc, x, centres, sigmas, w1, b1, out):
             phi_grouped = work.tile(
                 [P, len(tiles) * P, PACK], BF16, align_bytes=64, name="phi_grouped"
             )
-            if tiles[0] in GG:
-                nc.gpsimd.tensor_scalar(
-                    out=phi_grouped[:],
-                    in0=phi_blocks[:].rearrange("p t i -> p i t"),
-                    scalar1=-FLT_MAX,
-                    scalar2=1.0,
-                    op0=ALU.max,
-                    op1=ALU.min,
-                )
-            else:
-                nc.vector.tensor_scalar_min(
-                    out=phi_grouped[:], in0=phi_blocks[:].rearrange("p t i -> p i t"), scalar1=1.0
-                )
+            nc.vector.tensor_scalar_min(
+                out=phi_grouped[:], in0=phi_blocks[:].rearrange("p t i -> p i t"), scalar1=1.0
+            )
             return phi_grouped
 
         def quantise_phi(phi_grouped, tiles):
@@ -190,8 +181,8 @@ def tile_networkprc_pa_kernel(tc, x, centres, sigmas, w1, b1, out):
 
         def group_w(copy_out, q, pair, w_ps):
             copy_out(
-                out=w_grouped[q][:, pair * 2 * P : (pair + 1) * 2 * P, :],
-                in_=w_ps[:].rearrange("p u n -> p n u"),
+                out=w_grouped[q][:, pair * 2 * P : (pair + 1) * 2 * P, :].rearrange("p (r m) u -> p r m u", m=2),
+                in_=w_ps[:].rearrange("p u (m r) -> p r m u", m=2),
             )
 
         def quantise_w(q, first, columns):
@@ -258,17 +249,17 @@ def tile_networkprc_pa_kernel(tc, x, centres, sigmas, w1, b1, out):
         nc.sync.dma_start(out=c_sb[:], in_=centres.rearrange("(p t) k -> p t k", t=PACK))
         load_x(0, 2)
         nc.sync.dma_start(out=sig[:], in_=sigmas.rearrange("(p t) -> p t", t=PACK))
-        load_w(0, 0, 2)
+        load_w(0, 0, 1)
         nc.vector.memset(warm[:], 0.0)
         for half in range(2):
             cols = slice(half * CENT // 2, (half + 1) * CENT // 2)
             nc.vector.memset(b_row[half][:].bitcast(U32), 0)
             nc.sync.dma_start(out=b_row[half][0:1, :], in_=b1[cols].rearrange("(o n) -> o n", o=1))
             if half == 0:
-                load_w(0, 2, 2)
+                load_w(0, 1, 1)
                 load_x(2, 6)
         for q in range(1, CHUNKS):
-            load_w(q, 0, 4)
+            load_w(q, 0, 2)
 
         make_identity(nc, ident_bf[:])
         make_identity(nc, ident_f32[:])
@@ -286,6 +277,8 @@ def tile_networkprc_pa_kernel(tc, x, centres, sigmas, w1, b1, out):
         for t in range(PACK):
             nc.tensor.transpose(c_ps[:, t, :], c_sb[:, t, :], ident_bf[:])
         first_ps = transpose_x([0, 1])
+        for columns in D2:
+            warm_up(columns)
         w_a = transpose_w(0, 0)
         b_ps = spread_b(0)
 
@@ -344,14 +337,14 @@ def tile_networkprc_pa_kernel(tc, x, centres, sigmas, w1, b1, out):
             lambda: make_w(1, 1),
             lambda: make_phi(2),
             lambda: make_phi(3),
-            lambda: make_w(2, 0),
-            lambda: make_w(2, 1),
             lambda: make_phi(4),
+            lambda: make_w(2, 0),
             lambda: make_phi(5),
-            lambda: make_w(3, 0),
-            lambda: make_w(3, 1),
+            lambda: make_w(2, 1),
             lambda: make_phi(6),
+            lambda: make_w(3, 0),
             lambda: make_phi(7),
+            lambda: make_w(3, 1),
         ]
 
         def start_job(slot):
@@ -361,9 +354,9 @@ def tile_networkprc_pa_kernel(tc, x, centres, sigmas, w1, b1, out):
 
         for slot in range(-AHEAD, 0):
             start_job(slot)
-        order = [(0, 0), (1, 0), (0, 1), (1, 1)] + [(a, q) for a in (2, 3) for q in (0, 1)]
-        order += [(a, 2) for a in range(4)] + [(a, q) for a in (4, 5) for q in range(3)]
-        order += [(a, 3) for a in range(6)] + [(a, q) for a in (6, 7) for q in range(4)]
+        order = [(0, 0), (1, 0), (0, 1), (1, 1)] + [(a, q) for a in range(2, ROW_TILES) for q in (0, 1)]
+        order += [(a, q) for a in range(ROW_TILES) for q in (2, 3)]
+        pairs = {}
         for slot, (a, q) in enumerate(order):
             for stage in late.pop(slot, []):
                 stage()
@@ -371,15 +364,19 @@ def tile_networkprc_pa_kernel(tc, x, centres, sigmas, w1, b1, out):
             if slot < 2 or slot % 2 == 1:
                 for i in range(1 if slot < 2 else 2):
                     start_job(slot)
-            o_sb = work.tile([P, BANK], F32, bufs=OB, name="o_sb")
+            if (a, q // 2) not in pairs:
+                pairs[a, q // 2] = work.tile([P, 2, BANK], F32, bufs=OB, name="o_sb")
+            o_sb = pairs[a, q // 2][:, q % 2, :]
             cols = slice(q * BANK, (q + 1) * BANK)
-            nc.vector.tensor_tensor(out=o_sb[:], in0=acc[:], in1=b_all[:, cols], op=ALU.add)
+            nc.vector.tensor_tensor(out=o_sb, in0=acc[:], in1=b_all[:, cols], op=ALU.add)
             if RELU[slot] == "G":
                 nc.gpsimd.tensor_scalar(
-                    out=o_sb[:], in0=o_sb[:], scalar1=FLT_MAX, scalar2=0.0, op0=ALU.min, op1=ALU.max
+                    out=o_sb, in0=o_sb, scalar1=FLT_MAX, scalar2=0.0, op0=ALU.min, op1=ALU.max
                 )
             elif RELU[slot] == "V":
-                nc.vector.tensor_scalar_max(out=o_sb[:], in0=o_sb[:], scalar1=0.0)
+                nc.vector.tensor_scalar_max(out=o_sb, in0=o_sb, scalar1=0.0)
             else:
-                nc.scalar.activation(out=o_sb[:], in_=o_sb[:], func=ACT.Relu)
-            nc.sync.dma_start(out=out_view[:, a, cols], in_=o_sb[:])
+                nc.scalar.activation(out=o_sb, in_=o_sb, func=ACT.Relu)
+            if q % 2 == 1:
+                cols = slice((q - 1) * BANK, (q + 1) * BANK)
+                nc.sync.dma_start(out=out_view[:, a, cols], in_=pairs[a, q // 2][:].rearrange("p h n -> p (h n)"))

@@ -21,15 +21,19 @@ COL_TILES = BANK // P
 WORDS = HID // 2
 FLT_MAX = 3.4028234663852886e38
 
-D1 = (128, 128, 128, 128)
+D1 = (128, 128, 128)
 D2 = (128,)
 GB = 2
 OB = 8
 MXB = 4
-RELU = "GGGGGGGGGSGSGSGSGSGSGSGSGSGSGSGS"
+RELU = "GGGGGGSGSGSGSGSGSGSGSGSGSGSGSGSG"
 AHEAD = 2
 LAG = 2
 TPB = 2
+STARTS = {0: 1, 1: 1, 3: 2, 5: 2, 9: 1, 13: 1, 17: 1, 21: 1}
+FIRSTG = 8
+GL0 = 3
+GL1 = 4
 FLOPS = 2 * BATCH * IN * HID + 2 * BATCH * HID * CENT
 
 
@@ -88,7 +92,7 @@ def tile_networkprc_pa_kernel(tc, x, centres, sigmas, w1, b1, out):
             )
 
         def transpose_x(tiles):
-            x_ps = psum.tile([P, len(tiles), P], BF16, tag="tp", bufs=TPB, name="x_ps")
+            x_ps = psum.tile([P, len(tiles), P], BF16, tag="mx", bufs=MXB, name="x_ps")
             for i, a in enumerate(tiles):
                 nc.tensor.transpose(x_ps[:, i, :], x_sb[:, a, :], ident_bf[:])
             return x_ps
@@ -337,46 +341,59 @@ def tile_networkprc_pa_kernel(tc, x, centres, sigmas, w1, b1, out):
             lambda: make_w(1, 1),
             lambda: make_phi(2),
             lambda: make_phi(3),
-            lambda: make_phi(4),
             lambda: make_w(2, 0),
-            lambda: make_phi(5),
             lambda: make_w(2, 1),
-            lambda: make_phi(6),
             lambda: make_w(3, 0),
-            lambda: make_phi(7),
             lambda: make_w(3, 1),
+            lambda: make_phi(4),
+            lambda: make_phi(5),
+            lambda: make_phi(6),
+            lambda: make_phi(7),
         ]
 
         def start_job(slot):
             if jobs:
-                for i, stage in enumerate(jobs.pop(0)()):
-                    late.setdefault(slot + LAG + i, []).append(stage)
+                stages = jobs.pop(0)()
+                count = len(stages)
+                for i, stage in enumerate(stages):
+                    lag = LAG + i if slot < FIRSTG or count == 1 else (GL0, GL1)[i]
+                    late.setdefault(slot + lag, []).append(stage)
 
         for slot in range(-AHEAD, 0):
             start_job(slot)
-        order = [(0, 0), (1, 0), (0, 1), (1, 1)] + [(a, q) for a in range(2, ROW_TILES) for q in (0, 1)]
-        order += [(a, q) for a in range(ROW_TILES) for q in (2, 3)]
+        order = [(0, 0), (1, 0), (0, 1), (1, 1)] + [(a, q) for a in (2, 3) for q in (0, 1)]
+        order += [(a, q) for a in range(4) for q in (2, 3)] + [(a, q) for a in range(4, 8) for q in range(4)]
         pairs = {}
         for slot, (a, q) in enumerate(order):
             for stage in late.pop(slot, []):
                 stage()
             acc = product(a, q)
-            if slot < 2 or slot % 2 == 1:
-                for i in range(1 if slot < 2 else 2):
+            if slot in STARTS:
+                for i in range(STARTS[slot]):
                     start_job(slot)
-            if (a, q // 2) not in pairs:
-                pairs[a, q // 2] = work.tile([P, 2, BANK], F32, bufs=OB, name="o_sb")
-            o_sb = pairs[a, q // 2][:, q % 2, :]
-            cols = slice(q * BANK, (q + 1) * BANK)
-            nc.vector.tensor_tensor(out=o_sb, in0=acc[:], in1=b_all[:, cols], op=ALU.add)
-            if RELU[slot] == "G":
-                nc.gpsimd.tensor_scalar(
-                    out=o_sb, in0=o_sb, scalar1=FLT_MAX, scalar2=0.0, op0=ALU.min, op1=ALU.max
+            if q % 2 == 0:
+                o_sb = work.tile([P, 2, BANK], F32, bufs=OB, name="o_sb")
+                pairs[a] = o_sb
+            o_sb = pairs[a]
+            parts = 2 if slot == len(order) - 1 else 1
+            width = BANK // parts
+            for part in range(parts):
+                piece = o_sb[:, q % 2, part * width : (part + 1) * width]
+                c0 = q * BANK + part * width
+                nc.vector.tensor_tensor(
+                    out=piece, in0=acc[:, part * width : (part + 1) * width], in1=b_all[:, c0 : c0 + width], op=ALU.add
                 )
-            elif RELU[slot] == "V":
-                nc.vector.tensor_scalar_max(out=o_sb, in0=o_sb, scalar1=0.0)
-            else:
-                nc.scalar.activation(out=o_sb, in_=o_sb, func=ACT.Relu)
-            if q % 2 == 1:
-                cols = slice((q - 1) * BANK, (q + 1) * BANK)
-                nc.sync.dma_start(out=out_view[:, a, cols], in_=pairs[a, q // 2][:].rearrange("p h n -> p (h n)"))
+                if part == 1:
+                    nc.vector.tensor_scalar_max(out=piece, in0=piece, scalar1=0.0)
+                elif RELU[slot] == "G":
+                    nc.gpsimd.tensor_scalar(
+                        out=piece, in0=piece, scalar1=FLT_MAX, scalar2=0.0, op0=ALU.min, op1=ALU.max
+                    )
+                else:
+                    nc.scalar.activation(out=piece, in_=piece, func=ACT.Relu)
+                if slot >= len(order) - 2:
+                    nc.sync.dma_start(out=out_view[:, a, c0 : c0 + width], in_=piece)
+            if q % 2 == 1 and slot < len(order) - 2:
+                nc.sync.dma_start(
+                    out=out_view[:, a, (q - 1) * BANK : (q + 1) * BANK], in_=o_sb[:].rearrange("p h n -> p (h n)")
+                )

@@ -30,8 +30,8 @@ RELU = "GGGGGGSGSGSGSGSGSGSGSGSGSGSGSGSG"
 AHEAD = 2
 LAG = 2
 TPB = 2
-STARTS = {0: 1, 1: 1, 3: 2, 5: 2, 9: 1, 13: 1, 17: 1, 21: 1}
-FIRSTG = 8
+STARTS = {0: 1, 1: 1, 3: 2, 5: 2, 6: 1, 10: 1, 14: 1, 18: 1}
+FIRSTG = 6
 GL0 = 3
 GL1 = 4
 FLOPS = 2 * BATCH * IN * HID + 2 * BATCH * HID * CENT
@@ -69,6 +69,9 @@ def tile_networkprc_pa_kernel(tc, x, centres, sigmas, w1, b1, out):
         b_all = keep.tile([P, CENT], BF16)
         phi_codes = keep.tile([P, BATCH], U32, align_bytes=64)
         phi_scales = keep.tile([P, BATCH], U8, align_bytes=64)
+        o_last = keep.tile([P, COL_TILES, BANK], F32)
+        b_col = keep.tile([P, COL_TILES], F32)
+        o_turned = keep.tile([P, COL_TILES, COL_TILES, BANK // COL_TILES], F32)
         w_codes = keep.tile([P, CENT], U32, align_bytes=64)
         w_scales = keep.tile([P, CENT], U8, align_bytes=64)
         w_grouped = [
@@ -209,6 +212,46 @@ def tile_networkprc_pa_kernel(tc, x, centres, sigmas, w1, b1, out):
             copy_out(
                 out=b_all[:, half * CENT // 2 : (half + 1) * CENT // 2], in_=b_ps[:].rearrange("p i n -> p (i n)")
             )
+
+        def turn_b():
+            ps = psum.tile([P, COL_TILES], F32, tag="tp", bufs=TPB, name="b_col_ps")
+            for m in range(COL_TILES):
+                nc.tensor.matmul(
+                    out=ps[:, m : m + 1],
+                    lhsT=b_row[1][:, BANK + m * P : BANK + (m + 1) * P],
+                    rhs=ones_bf[:, 0:1],
+                    start=True,
+                    stop=True,
+                )
+            nc.scalar.copy(out=b_col[:], in_=ps[:])
+
+        def turned_product(m):
+            acc = psum.tile([P, BANK], F32, tag="mx", bufs=MXB, name="acc")
+            cols = slice(3 * BANK + m * P, 3 * BANK + (m + 1) * P)
+            nc.tensor.matmul_mx(
+                out=acc[:],
+                lhsT=w_codes[:, cols].bitcast(FP8X4),
+                lhsT_scale=w_scales[:, cols],
+                rhs=phi_codes[:, 0:BANK].bitcast(FP8X4),
+                rhs_scale=phi_scales[:, 0:BANK],
+                start=True,
+                stop=True,
+            )
+            nc.scalar.activation(
+                out=o_turned[:, m, :, :].rearrange("p a r -> p (a r)"),
+                in_=acc[:],
+                func=ACT.Relu,
+                bias=b_col[:, m : m + 1],
+            )
+
+        def turn_back(m):
+            ps = psum.tile([P, COL_TILES, P], F32, tag="tp", bufs=TPB, name="turn_ps")
+            for a in range(COL_TILES):
+                nc.tensor.transpose(ps[:, a, :], o_turned[:, m, a, :], ident_f32[:])
+            return ps
+
+        def keep_turned(m, ps):
+            nc.scalar.copy(out=o_last[:, :, m * P : (m + 1) * P], in_=ps[:])
 
         def product(a, q):
             acc = psum.tile([P, BANK], F32, tag="mx", bufs=MXB, name="acc")
@@ -362,19 +405,32 @@ def tile_networkprc_pa_kernel(tc, x, centres, sigmas, w1, b1, out):
         for slot in range(-AHEAD, 0):
             start_job(slot)
         order = [(0, 0), (1, 0), (0, 1), (1, 1)] + [(a, q) for a in (2, 3) for q in (0, 1)]
-        order += [(a, q) for a in range(4) for q in (2, 3)] + [(a, q) for a in range(4, 8) for q in range(4)]
+        order += [(a, 2) for a in range(4)]
+        order += [(a, q) for a in range(4, 8) for q in range(4)]
         pairs = {}
+        extra = {}
+
+        def plan_turned(m, slot):
+            made = []
+            extra.setdefault(slot, []).append(lambda: turned_product(m))
+            extra.setdefault(slot + 4, []).append(lambda: made.append(turn_back(m)))
+            extra.setdefault(slot + 5, []).append(lambda: keep_turned(m, made[0]))
+
+        extra[7] = [turn_b]
+        for m in range(COL_TILES):
+            plan_turned(m, 8 + 4 * m)
         for slot, (a, q) in enumerate(order):
             for stage in late.pop(slot, []):
                 stage()
             acc = product(a, q)
+            for step in extra.get(slot, []):
+                step()
             if slot in STARTS:
                 for i in range(STARTS[slot]):
                     start_job(slot)
-            if q % 2 == 0:
-                o_sb = work.tile([P, 2, BANK], F32, bufs=OB, name="o_sb")
-                pairs[a] = o_sb
-            o_sb = pairs[a]
+            if (a, q // 2) not in pairs:
+                pairs[a, q // 2] = work.tile([P, 2, BANK], F32, bufs=OB, name="o_sb")
+            o_sb = pairs[a, q // 2]
             parts = 2 if slot == len(order) - 1 else 1
             width = BANK // parts
             for part in range(parts):
@@ -391,9 +447,12 @@ def tile_networkprc_pa_kernel(tc, x, centres, sigmas, w1, b1, out):
                     )
                 else:
                     nc.scalar.activation(out=piece, in_=piece, func=ACT.Relu)
-                if slot >= len(order) - 2:
+                if slot >= len(order) - 2 or (a < 4 and q == 2):
                     nc.sync.dma_start(out=out_view[:, a, c0 : c0 + width], in_=piece)
             if q % 2 == 1 and slot < len(order) - 2:
                 nc.sync.dma_start(
                     out=out_view[:, a, (q - 1) * BANK : (q + 1) * BANK], in_=o_sb[:].rearrange("p h n -> p (h n)")
                 )
+            if slot in (13, 17, 21, 25):
+                c0 = (slot - 13) // 4 * P
+                nc.sync.dma_start(out=out_view[:, 0:4, 3 * BANK + c0 : 3 * BANK + c0 + P], in_=o_last[:, :, c0 : c0 + P])

@@ -21,7 +21,7 @@ COL_TILES = BANK // P
 WORDS = HID // 2
 FLT_MAX = 3.4028234663852886e38
 
-D1 = (128, 128, 128)
+D1 = (128, 128, 128, 128)
 D2 = (128,)
 GB = 2
 OB = 8
@@ -376,7 +376,15 @@ def tile_networkprc_pa_kernel(tc, x, centres, sigmas, w1, b1, out):
             norm_x(a)
         copy_b(nc.scalar.copy, 1, b1_ps)
         copy_xT(rest_ps, list(range(2, ROW_TILES)))
-        spread_norms(2, 6)
+        spread_norms(2, 2)
+        nc.gpsimd.tensor_scalar(
+            out=x_rep[:, 4 : 8, :],
+            in0=x_norm[:, 4 : 8].unsqueeze(2).to_broadcast([P, 4, P]),
+            scalar1=1.0,
+            scalar2=0.0,
+            op0=ALU.mult,
+            op1=ALU.add,
+        )
         late = {1: [lambda: quantise_phi(g1, [1])]}
 
         jobs = [
@@ -413,8 +421,8 @@ def tile_networkprc_pa_kernel(tc, x, centres, sigmas, w1, b1, out):
         def plan_turned(m, slot):
             made = []
             extra.setdefault(slot, []).append(lambda: turned_product(m))
-            extra.setdefault(slot + 4, []).append(lambda: made.append(turn_back(m)))
-            extra.setdefault(slot + 5, []).append(lambda: keep_turned(m, made[0]))
+            extra.setdefault(slot + 3, []).append(lambda: made.append(turn_back(m)))
+            extra.setdefault(slot + 4, []).append(lambda: keep_turned(m, made[0]))
 
         extra[7] = [turn_b]
         for m in range(COL_TILES):
@@ -447,12 +455,12 @@ def tile_networkprc_pa_kernel(tc, x, centres, sigmas, w1, b1, out):
                     )
                 else:
                     nc.scalar.activation(out=piece, in_=piece, func=ACT.Relu)
-                if slot >= len(order) - 2 or (a < 4 and q == 2):
+                if slot < 8 or slot >= len(order) - 2 or (a < 4 and q == 2):
                     nc.sync.dma_start(out=out_view[:, a, c0 : c0 + width], in_=piece)
-            if q % 2 == 1 and slot < len(order) - 2:
+            if q % 2 == 1 and 8 <= slot < len(order) - 2:
                 nc.sync.dma_start(
                     out=out_view[:, a, (q - 1) * BANK : (q + 1) * BANK], in_=o_sb[:].rearrange("p h n -> p (h n)")
                 )
-            if slot in (13, 17, 21, 25):
-                c0 = (slot - 13) // 4 * P
+            if slot in (12, 16, 20, 24):
+                c0 = (slot - 12) // 4 * P
                 nc.sync.dma_start(out=out_view[:, 0:4, 3 * BANK + c0 : 3 * BANK + c0 + P], in_=o_last[:, :, c0 : c0 + P])

@@ -22,7 +22,7 @@ WORDS = HID // 2
 FLT_MAX = 3.4028234663852886e38
 
 D1 = (128, 128, 128, 128)
-D2 = (128,)
+D2 = (128, 128)
 GB = 2
 OB = 8
 MXB = 4
@@ -295,8 +295,8 @@ def tile_networkprc_pa_kernel(tc, x, centres, sigmas, w1, b1, out):
 
         nc.sync.dma_start(out=c_sb[:], in_=centres.rearrange("(p t) k -> p t k", t=PACK))
         load_x(0, 2)
-        nc.sync.dma_start(out=sig[:], in_=sigmas.rearrange("(p t) -> p t", t=PACK))
         load_w(0, 0, 1)
+        nc.sync.dma_start(out=sig[:], in_=sigmas.rearrange("(p t) -> p t", t=PACK))
         nc.vector.memset(warm[:], 0.0)
         for half in range(2):
             cols = slice(half * CENT // 2, (half + 1) * CENT // 2)
@@ -374,7 +374,6 @@ def tile_networkprc_pa_kernel(tc, x, centres, sigmas, w1, b1, out):
         g1 = group_phi(e1, [1])
         for a in range(4, ROW_TILES):
             norm_x(a)
-        copy_b(nc.scalar.copy, 1, b1_ps)
         copy_xT(rest_ps, list(range(2, ROW_TILES)))
         spread_norms(2, 2)
         nc.gpsimd.tensor_scalar(
@@ -433,6 +432,8 @@ def tile_networkprc_pa_kernel(tc, x, centres, sigmas, w1, b1, out):
             acc = product(a, q)
             for step in extra.get(slot, []):
                 step()
+            if slot == 0:
+                copy_b(nc.scalar.copy, 1, b1_ps)
             if slot in STARTS:
                 for i in range(STARTS[slot]):
                     start_job(slot)

from contextlib import ExitStack

import concourse.mybir as mybir
from concourse.masks import make_identity

F32 = mybir.dt.float32
BF16 = mybir.dt.bfloat16
U32 = mybir.dt.uint32
U8 = mybir.dt.uint8
FP8X4 = mybir.dt.float8_e4m3fn_x4
ALU = mybir.AluOpType
ACT = mybir.ActivationFunctionType

P = 128
PACK = 4
BATCH, IN, HID, CENT = 1024, 128, 512, 2048
BANK = 512
ROW_TILES = BATCH // P
CHUNKS = CENT // BANK
COL_TILES = BANK // P
WORDS = HID // 2
FLT_MAX = 3.4028234663852886e38

D1 = (128, 128, 128, 128)
D2 = (128, 128)
GB = 2
OB = 8
MXB = 4
RELU = "GGGGGGSGSGSGSGSGSGSGSGSGSGSGSGSG"
AHEAD = 2
LAG = 2
TPB = 2
STARTS = {0: 1, 1: 1, 3: 2, 5: 2, 6: 1, 10: 1, 14: 1, 18: 1}
FIRSTG = 6
GL0 = 3
GL1 = 4
FLOPS = 2 * BATCH * IN * HID + 2 * BATCH * HID * CENT


def tile_networkprc_pa_kernel(tc, x, centres, sigmas, w1, b1, out):
    nc = tc.nc
    with ExitStack() as ctx:
        keep = ctx.enter_context(tc.tile_pool(name="keep", bufs=1))
        work = ctx.enter_context(tc.tile_pool(name="work", bufs=2))
        psum = ctx.enter_context(tc.psum_pool(name="psum", bufs=2))
        ctx.enter_context(tc.manual_schedule())

        c_sb = keep.tile([P, PACK, IN], BF16)
        x_sb = keep.tile([P, ROW_TILES, IN], BF16)
        sig = keep.tile([P, PACK], BF16)
        b_row = [keep.tile([P, CENT // 2], BF16, name="b_row%d" % half) for half in range(2)]
        warm = keep.tile([P, P], F32)
        w_sb = [keep.tile([P, COL_TILES * HID], BF16, name="w_sb%d" % q) for q in range(CHUNKS)]
        ident_bf = keep.tile([P, P], BF16)
        ident_f32 = keep.tile([P, P], F32)
        ones_bf = keep.tile([P, P], BF16)
        zero_col = keep.tile([P, 1], F32)
        one_col = keep.tile([P, 1], F32)
        cT = keep.tile([P, PACK, P], BF16)
        xT = keep.tile([P, BATCH], BF16)
        sq_c = keep.tile([P, PACK, IN], F32)
        sq_x = keep.tile([P, ROW_TILES, IN], F32)
        c_norm_v = keep.tile([P, 1], F32)
        c_norm_s = keep.tile([P, PACK], F32)
        x_norm = keep.tile([P, ROW_TILES], F32)
        x_rep = keep.tile([P, ROW_TILES, P], F32)
        exp_scale = keep.tile([P, PACK], F32)
        exp_bias = keep.tile([P, PACK], F32)
        b_all = keep.tile([P, CENT], BF16)
        phi_codes = keep.tile([P, BATCH], U32, align_bytes=64)
        phi_scales = keep.tile([P, BATCH], U8, align_bytes=64)
        o_last = keep.tile([P, COL_TILES, BANK], F32)
        b_col = keep.tile([P, COL_TILES], F32)
        o_turned = keep.tile([P, COL_TILES, COL_TILES, BANK // COL_TILES], F32)
        w_codes = keep.tile([P, CENT], U32, align_bytes=64)
        w_scales = keep.tile([P, CENT], U8, align_bytes=64)
        w_grouped = [
            keep.tile([P, BANK, 2], F32, align_bytes=64, name="w_grouped%d" % q) for q in range(CHUNKS)
        ]
        out_view = out.rearrange("(p a) n -> p a n", a=ROW_TILES)

        def load_w(q, first_pair, pairs):
            c0 = q * BANK + first_pair * 2 * P
            nc.sync.dma_start(
                out=w_sb[q][:, first_pair * 2 * HID : (first_pair + pairs) * 2 * HID].rearrange(
                    "p (h m k) -> p h m k", m=2, k=HID
                ),
                in_=w1[c0 : c0 + pairs * 2 * P, :].rearrange("(h p m) k -> p h m k", p=P, m=2),
            )

        def load_x(first_tile, tiles):
            nc.sync.dma_start(
                out=x_sb[:, first_tile : first_tile + tiles, :],
                in_=x.rearrange("(p a) k -> p a k", a=ROW_TILES)[:, first_tile : first_tile + tiles, :],
            )

        def transpose_x(tiles):
            x_ps = psum.tile([P, len(tiles), P], BF16, tag="mx", bufs=MXB, name="x_ps")
            for i, a in enumerate(tiles):
                nc.tensor.transpose(x_ps[:, i, :], x_sb[:, a, :], ident_bf[:])
            return x_ps

        def copy_xT(x_ps, tiles):
            nc.vector.tensor_copy(
                out=xT[:, tiles[0] * P : (tiles[-1] + 1) * P], in_=x_ps[:].rearrange("p a r -> p (a r)")
            )

        def norm_x(a):
            nc.scalar.activation(
                out=sq_x[:, a, :], in_=x_sb[:, a, :], func=ACT.Square, accum_out=x_norm[:, a : a + 1]
            )

        def spread_norms(first, tiles):
            nc.vector.tensor_copy(
                out=x_rep[:, first : first + tiles, :],
                in_=x_norm[:, first : first + tiles].unsqueeze(2).to_broadcast([P, tiles, P]),
            )

        def distances(tiles):
            rows = len(tiles) * P
            blocks = BANK // rows
            banks = []
            for first in range(0, PACK, blocks):
                d_ps = psum.tile([P, blocks, rows], F32, tag="g", name="d_ps")
                for i in range(blocks):
                    nc.tensor.matmul(
                        out=d_ps[:, i, :],
                        lhsT=cT[:, first + i, :],
                        rhs=xT[:, tiles[0] * P : (tiles[-1] + 1) * P],
                        start=True,
                        stop=False,
                    )
                    for j, a in enumerate(tiles):
                        nc.tensor.matmul(
                            out=d_ps[:, i, j * P : (j + 1) * P],
                            lhsT=x_rep[:, a, :],
                            rhs=ident_f32[:],
                            is_transpose=True,
                            start=False,
                            stop=a == tiles[-1],
                        )
                banks.append(d_ps)
            return banks

        def exps(banks, tiles):
            rows = len(tiles) * P
            blocks = BANK // rows
            phi_blocks = work.tile([P, PACK, rows], BF16, bufs=4, name="phi_blocks%d" % len(tiles))
            for t in range(PACK):
                nc.scalar.activation(
                    out=phi_blocks[:, t, :],
                    in_=banks[t // blocks][:, t % blocks, :],
                    func=ACT.Exp,
                    scale=exp_scale[:, t : t + 1],
                    bias=exp_bias[:, t : t + 1],
                )
            return phi_blocks

        def group_phi(phi_blocks, tiles):
            phi_grouped = work.tile(
                [P, len(tiles) * P, PACK], BF16, align_bytes=64, name="phi_grouped"
            )
            nc.vector.tensor_scalar_min(
                out=phi_grouped[:], in0=phi_blocks[:].rearrange("p t i -> p i t"), scalar1=1.0
            )
            return phi_grouped

        def quantise_phi(phi_grouped, tiles):
            rows = slice(tiles[0] * P, (tiles[-1] + 1) * P)
            nc.vector.quantize_mx(
                out=phi_codes[:, rows].bitcast(FP8X4),
                scales=phi_scales[:, rows],
                in_=phi_grouped[:].rearrange("p i t -> p (i t)"),
            )

        def transpose_w(q, pair):
            words = w_sb[q][:].bitcast(F32)
            w_ps = psum.tile([P, 2, 2 * P], F32, tag="tp", bufs=TPB, name="w_ps")
            for u in range(2):
                for half in range(2):
                    m = 2 * pair + half
                    nc.tensor.transpose(
                        w_ps[:, u, half * P : (half + 1) * P],
                        words[:, m * WORDS + u : (m + 1) * WORDS : 2],
                        ident_f32[:],
                    )
            return w_ps

        def group_w(copy_out, q, pair, w_ps):
            copy_out(
                out=w_grouped[q][:, pair * 2 * P : (pair + 1) * 2 * P, :].rearrange("p (r m) u -> p r m u", m=2),
                in_=w_ps[:].rearrange("p u (m r) -> p r m u", m=2),
            )

        def quantise_w(q, first, columns):
            cols = slice(q * BANK + first, q * BANK + first + columns)
            nc.vector.quantize_mx(
                out=w_codes[:, cols].bitcast(FP8X4),
                scales=w_scales[:, cols],
                in_=w_grouped[q][:, first : first + columns, :].rearrange("p n u -> p (n u)").bitcast(BF16),
            )

        def spread_b(half):
            b_ps = psum.tile([P, 2, BANK], BF16, tag="mx", bufs=MXB, name="b_ps")
            for i in range(2):
                nc.tensor.matmul(
                    out=b_ps[:, i, :], lhsT=ones_bf[:], rhs=b_row[half][:, i * BANK : (i + 1) * BANK], start=True, stop=True
                )
            return b_ps

        def copy_b(copy_out, half, b_ps):
            copy_out(
                out=b_all[:, half * CENT // 2 : (half + 1) * CENT // 2], in_=b_ps[:].rearrange("p i n -> p (i n)")
            )

        def turn_b():
            ps = psum.tile([P, COL_TILES], F32, tag="tp", bufs=TPB, name="b_col_ps")
            for m in range(COL_TILES):
                nc.tensor.matmul(
                    out=ps[:, m : m + 1],
                    lhsT=b_row[1][:, BANK + m * P : BANK + (m + 1) * P],
                    rhs=ones_bf[:, 0:1],
                    start=True,
                    stop=True,
                )
            nc.scalar.copy(out=b_col[:], in_=ps[:])

        def turned_product(m):
            acc = psum.tile([P, BANK], F32, tag="mx", bufs=MXB, name="acc")
            cols = slice(3 * BANK + m * P, 3 * BANK + (m + 1) * P)
            nc.tensor.matmul_mx(
                out=acc[:],
                lhsT=w_codes[:, cols].bitcast(FP8X4),
                lhsT_scale=w_scales[:, cols],
                rhs=phi_codes[:, 0:BANK].bitcast(FP8X4),
                rhs_scale=phi_scales[:, 0:BANK],
                start=True,
                stop=True,
            )
            nc.scalar.activation(
                out=o_turned[:, m, :, :].rearrange("p a r -> p (a r)"),
                in_=acc[:],
                func=ACT.Relu,
                bias=b_col[:, m : m + 1],
            )

        def turn_back(m):
            ps = psum.tile([P, COL_TILES, P], F32, tag="tp", bufs=TPB, name="turn_ps")
            for a in range(COL_TILES):
                nc.tensor.transpose(ps[:, a, :], o_turned[:, m, a, :], ident_f32[:])
            return ps

        def keep_turned(m, ps):
            nc.scalar.copy(out=o_last[:, :, m * P : (m + 1) * P], in_=ps[:])

        def product(a, q):
            acc = psum.tile([P, BANK], F32, tag="mx", bufs=MXB, name="acc")
            rows = slice(a * P, (a + 1) * P)
            cols = slice(q * BANK, (q + 1) * BANK)
            nc.tensor.matmul_mx(
                out=acc[:],
                lhsT=phi_codes[:, rows].bitcast(FP8X4),
                lhsT_scale=phi_scales[:, rows],
                rhs=w_codes[:, cols].bitcast(FP8X4),
                rhs_scale=w_scales[:, cols],
                start=True,
                stop=True,
            )
            return acc

        def add_b(o_sb, j, q, acc):
            nc.vector.tensor_tensor(
                out=o_sb[:, j, :], in0=acc[:], in1=b_all[:, q * BANK : (q + 1) * BANK], op=ALU.add
            )

        def relu(o_sb, j, engine):
            if engine == "G":
                nc.gpsimd.tensor_scalar(
                    out=o_sb[:, j, :], in0=o_sb[:, j, :], scalar1=FLT_MAX, scalar2=0.0, op0=ALU.min, op1=ALU.max
                )
            else:
                nc.scalar.activation(out=o_sb[:, j, :], in_=o_sb[:, j, :], func=ACT.Relu)

        def make_w(q, pair):
            group_w(nc.scalar.copy, q, pair, transpose_w(q, pair))
            if pair == 1:
                return [lambda: quantise_w(q, 0, BANK)]
            return []

        def make_phi(a):
            phi_blocks = exps(distances([a]), [a])
            grouped = []
            return [lambda: grouped.append(group_phi(phi_blocks, [a])), lambda: quantise_phi(grouped[0], [a])]


        nc.sync.dma_start(out=c_sb[:], in_=centres.rearrange("(p t) k -> p t k", t=PACK))
        load_x(0, 2)
        load_w(0, 0, 1)
        nc.sync.dma_start(out=sig[:], in_=sigmas.rearrange("(p t) -> p t", t=PACK))
        nc.vector.memset(warm[:], 0.0)
        for half in range(2):
            cols = slice(half * CENT // 2, (half + 1) * CENT // 2)
            nc.vector.memset(b_row[half][:].bitcast(U32), 0)
            nc.sync.dma_start(out=b_row[half][0:1, :], in_=b1[cols].rearrange("(o n) -> o n", o=1))
            if half == 0:
                load_w(0, 1, 1)
                load_x(2, 6)
        for q in range(1, CHUNKS):
            load_w(q, 0, 2)

        make_identity(nc, ident_bf[:])
        make_identity(nc, ident_f32[:])
        nc.gpsimd.memset(zero_col[:], 0.0)
        nc.gpsimd.memset(ones_bf[:], 1.0)
        nc.scalar.activation(out=one_col[:], in_=zero_col[:], func=ACT.Exp)

        def warm_up(columns):
            w_ps = psum.tile([P, BANK], F32, tag="mx", bufs=MXB, name="warm_ps")
            nc.tensor.matmul(out=w_ps[:, 0:columns], lhsT=warm[:, 0:P], rhs=warm[:, 0:columns], start=True, stop=True)

        for columns in D1:
            warm_up(columns)
        c_ps = psum.tile([P, PACK, P], BF16, tag="tp", bufs=TPB)
        for t in range(PACK):
            nc.tensor.transpose(c_ps[:, t, :], c_sb[:, t, :], ident_bf[:])
        first_ps = transpose_x([0, 1])
        for columns in D2:
            warm_up(columns)
        w_a = transpose_w(0, 0)
        b_ps = spread_b(0)

        def norm_c_on_scalar(t):
            nc.scalar.activation(
                out=sq_c[:, t, :], in_=c_sb[:, t, :], func=ACT.Square, accum_out=c_norm_s[:, t : t + 1]
            )

        norm_c_on_scalar(1)
        norm_x(0)
        norm_x(1)
        norm_c_on_scalar(2)
        norm_c_on_scalar(3)
        nc.vector.scalar_tensor_tensor(
            out=sq_c[:, 0, :],
            in0=c_sb[:, 0, :],
            scalar=1.0,
            in1=c_sb[:, 0, :],
            op0=ALU.mult,
            op1=ALU.mult,
            accum_out=c_norm_v[:],
        )
        nc.vector.tensor_scalar(out=cT[:], in0=c_ps[:], scalar1=-2.0, scalar2=None, op0=ALU.mult)
        copy_xT(first_ps, [0, 1])
        spread_norms(0, 2)
        nc.vector.scalar_tensor_tensor(
            out=exp_scale[:], in0=sig[:], scalar=-1.0, in1=sig[:], op0=ALU.mult, op1=ALU.mult
        )
        nc.vector.tensor_tensor(out=exp_bias[:, 0:1], in0=exp_scale[:, 0:1], in1=c_norm_v[:], op=ALU.mult)
        nc.vector.tensor_tensor(out=exp_bias[:, 1:], in0=exp_scale[:, 1:], in1=c_norm_s[:, 1:], op=ALU.mult)

        e0 = exps(distances([0]), [0])
        group_w(nc.vector.tensor_copy, 0, 0, w_a)
        w_b = transpose_w(0, 1)
        copy_b(nc.vector.tensor_copy, 0, b_ps)
        quantise_w(0, 0, 256)
        norm_x(2)
        norm_x(3)
        e1 = exps(distances([1]), [1])
        g0 = group_phi(e0, [0])
        group_w(nc.vector.tensor_copy, 0, 1, w_b)
        quantise_phi(g0, [0])
        b1_ps = spread_b(1)
        quantise_w(0, 256, 256)
        rest_ps = transpose_x(list(range(2, ROW_TILES)))
        g1 = group_phi(e1, [1])
        for a in range(4, ROW_TILES):
            norm_x(a)
        copy_xT(rest_ps, list(range(2, ROW_TILES)))
        spread_norms(2, 2)
        nc.gpsimd.tensor_scalar(
            out=x_rep[:, 4 : 8, :],
            in0=x_norm[:, 4 : 8].unsqueeze(2).to_broadcast([P, 4, P]),
            scalar1=1.0,
            scalar2=0.0,
            op0=ALU.mult,
            op1=ALU.add,
        )
        late = {1: [lambda: quantise_phi(g1, [1])]}

        jobs = [
            lambda: make_w(1, 0),
            lambda: make_w(1, 1),
            lambda: make_phi(2),
            lambda: make_phi(3),
            lambda: make_w(2, 0),
            lambda: make_w(2, 1),
            lambda: make_w(3, 0),
            lambda: make_w(3, 1),
            lambda: make_phi(4),
            lambda: make_phi(5),
            lambda: make_phi(6),
            lambda: make_phi(7),
        ]

        def start_job(slot):
            if jobs:
                stages = jobs.pop(0)()
                count = len(stages)
                for i, stage in enumerate(stages):
                    lag = LAG + i if slot < FIRSTG or count == 1 else (GL0, GL1)[i]
                    late.setdefault(slot + lag, []).append(stage)

        for slot in range(-AHEAD, 0):
            start_job(slot)
        order = [(0, 0), (1, 0), (0, 1), (1, 1)] + [(a, q) for a in (2, 3) for q in (0, 1)]
        order += [(a, 2) for a in range(4)]
        order += [(a, q) for a in range(4, 8) for q in range(4)]
        pairs = {}
        extra = {}

        def plan_turned(m, slot):
            made = []
            extra.setdefault(slot, []).append(lambda: turned_product(m))
            extra.setdefault(slot + 3, []).append(lambda: made.append(turn_back(m)))
            extra.setdefault(slot + 4, []).append(lambda: keep_turned(m, made[0]))

        extra[7] = [turn_b]
        for m in range(COL_TILES):
            plan_turned(m, 8 + 4 * m)
        for slot, (a, q) in enumerate(order):
            for stage in late.pop(slot, []):
                stage()
            acc = product(a, q)
            for step in extra.get(slot, []):
                step()
            if slot == 0:
                copy_b(nc.scalar.copy, 1, b1_ps)
            if slot in STARTS:
                for i in range(STARTS[slot]):
                    start_job(slot)
            if (a, q // 2) not in pairs:
                pairs[a, q // 2] = work.tile([P, 2, BANK], F32, bufs=OB, name="o_sb")
            o_sb = pairs[a, q // 2]
            parts = 2 if slot == len(order) - 1 else 1
            width = BANK // parts
            for part in range(parts):
                piece = o_sb[:, q % 2, part * width : (part + 1) * width]
                c0 = q * BANK + part * width
                nc.vector.tensor_tensor(
                    out=piece, in0=acc[:, part * width : (part + 1) * width], in1=b_all[:, c0 : c0 + width], op=ALU.add
                )
                if part == 1:
                    nc.vector.tensor_scalar_max(out=piece, in0=piece, scalar1=0.0)
                elif RELU[slot] == "G":
                    nc.gpsimd.tensor_scalar(
                        out=piece, in0=piece, scalar1=FLT_MAX, scalar2=0.0, op0=ALU.min, op1=ALU.max
                    )
                else:
                    nc.scalar.activation(out=piece, in_=piece, func=ACT.Relu)
                if slot < 8 or slot >= len(order) - 2 or (a < 4 and q == 2):
                    nc.sync.dma_start(out=out_view[:, a, c0 : c0 + width], in_=piece)
            if q % 2 == 1 and 8 <= slot < len(order) - 2:
                nc.sync.dma_start(
                    out=out_view[:, a, (q - 1) * BANK : (q + 1) * BANK], in_=o_sb[:].rearrange("p h n -> p (h n)")
                )
            if slot in (12, 16, 20, 24):
                c0 = (slot - 12) // 4 * P
                nc.sync.dma_start(out=out_view[:, 0:4, 3 * BANK + c0 : 3 * BANK + c0 + P], in_=o_last[:, :, c0 : c0 + P])
